import numpy as np
import ml_dtypes


def mxq(x, axis, fmt="e4m3"):
    dtype, down = {"e4m3": (ml_dtypes.float8_e4m3fn, 7), "e5m2": (ml_dtypes.float8_e5m2, 14)}[fmt]
    v = np.moveaxis(np.asarray(x, np.float32).astype(ml_dtypes.bfloat16).astype(np.float64), axis, -1)
    blocks = v.reshape(v.shape[:-1] + (-1, 32))
    amax = np.abs(blocks).max(-1, keepdims=True)
    byte = np.maximum(np.where(amax > 0, np.frexp(amax)[1] - 1 + 127, 0) - down, 1)
    scale = np.exp2(byte - 127.0)
    codes = (blocks / scale).astype(np.float32).astype(dtype).astype(np.float64)
    return np.moveaxis((codes * scale).reshape(v.shape), -1, axis)


WIDE = False


def mx_kscale(k):
    if not WIDE:
        return np.ones(k)
    levels = np.array([10, -10, 5, -5, 0])
    if k % 512:
        return np.exp2(np.random.permutation(np.resize(levels, k // 32))).repeat(32)
    a = np.empty((k // 512, 16))
    for p in range(k // 512):
        a[p, :8] = np.random.permutation(np.resize(levels, 8))
        for g in range(8):
            far = levels[np.abs(levels - a[p, g]) >= 10]
            a[p, g + 8] = far[np.random.randint(len(far))]
    return np.exp2(a.ravel()).repeat(32)


BF16 = ml_dtypes.bfloat16


def bf(x):
    return np.asarray(x, np.float32).astype(BF16)


def f64(x):
    return np.asarray(x).astype(np.float64)


B, I, H, ORDER = 8192, 512, 256, 2
OH = ORDER * H


def sigmoid(v):
    return 1.0 / (1.0 + np.exp(-v))


def draw0():
    s, t = mx_kscale(I), mx_kscale(OH)
    return {"x": bf(np.random.standard_normal((B, I)) * s),
            "me_output": bf(np.random.standard_normal((B, OH)) * t),
            "W_memi": bf(np.random.standard_normal((I, OH)) * 0.7 / np.sqrt(I) / s[:, None]),
            "W_memh": bf(np.random.standard_normal((OH, OH)) * 0.7 / np.sqrt(OH) / t[:, None]),
            "W_memt": bf(np.random.standard_normal((OH, H)) * 1.0 / np.sqrt(OH) / t[:, None]),
            "mem_bias": bf(np.random.standard_normal(OH) * 0.3)}


def core(x, me_output, W_memi, W_memh, W_memt, mem_bias):
    me = f64(me_output)
    mg = ((mxq(f64(x), 1, "e4m3") @ mxq(f64(W_memi), 0, "e4m3"))
          + (mxq(me, 1, "e4m3") @ mxq(f64(W_memh), 0, "e4m3"))
          + f64(mem_bias))
    gated = sigmoid(mg) * me
    return mxq(gated, 1, "e4m3") @ mxq(f64(W_memt), 0, "e4m3")


def e4m3fn_bytes(y):
    return np.clip(np.asarray(y, np.float64), -448.0, 448.0).astype(np.float32).astype(ml_dtypes.float8_e4m3fn).view(np.uint8)


def e4m3fn_values(b):
    return np.asarray(b, np.uint8).view(ml_dtypes.float8_e4m3fn).astype(np.float64)


def setup_inputs():
    d = draw0()
    x0 = np.asarray(d['x']).astype(np.float64)
    s = (np.max(np.abs(x0), axis=(0,), keepdims=True) / 448.0).astype(np.float32)
    out = {}
    for k, v in d.items():
        if k == 'x':
            out['x_bytes'] = e4m3fn_bytes(x0 / s.astype(np.float64))
            out['x_scale'] = s
        else:
            out[k] = v
    return out


def reference(x_bytes, x_scale, me_output, W_memi, W_memh, W_memt, mem_bias):
    return core(e4m3fn_values(x_bytes) * x_scale.astype(np.float64), me_output, W_memi, W_memh, W_memt, mem_bias)

@@ -1,0 +1,283 @@
+from contextlib import ExitStack
+
+import concourse.mybir as mybir
+from concourse.masks import make_identity
+
+B, I, H, OH = 8192, 512, 256, 512
+FLOPS = 2 * B * I * OH + 2 * B * OH * OH + 2 * B * OH * H
+
+F32 = mybir.dt.float32
+BF16 = mybir.dt.bfloat16
+U32 = mybir.dt.uint32
+U8 = mybir.dt.uint8
+FP8 = mybir.dt.float8_e4m3fn
+FP8X4 = mybir.dt.float8_e4m3fn_x4
+MULT = mybir.AluOpType.mult
+SIGMOID = mybir.ActivationFunctionType.Sigmoid
+
+P = 128
+ROWS = B // P
+STEP_ROWS = 2
+STEPS = ROWS // STEP_ROWS
+N = STEP_ROWS * P
+CHUNK_STEPS = [1, 1, 2] + [4] * 7
+FIRST_CHUNKS = 4
+LOAD_LEAD = 10
+
+
+def tile_lstmcell_pa_t_kernel(tc, x_bytes, x_scale, me_output, W_memi, W_memh, W_memt, mem_bias, out):
+    nc = tc.nc
+    x_rows = x_bytes.rearrange("(p r) k -> p r k", p=P)
+    me_rows = me_output.rearrange("(p r) k -> p r k", p=P)
+    out_rows = out.rearrange("(p r) n -> p r n", p=P)
+
+    with ExitStack() as ctx:
+        keep = ctx.enter_context(tc.tile_pool(name="keep", bufs=1))
+        work = ctx.enter_context(tc.tile_pool(name="work", bufs=3))
+        psum = ctx.enter_context(tc.psum_pool(name="psum", bufs=1))
+        ctx.enter_context(tc.manual_schedule())
+
+        chunk_of = []
+        chunk_start = []
+        for c, n in enumerate(CHUNK_STEPS):
+            chunk_start.append(len(chunk_of))
+            chunk_of.extend([c] * n)
+        x_tiles = {}
+        me_tiles = {}
+
+        def load_x(c):
+            s0, n = chunk_start[c] * STEP_ROWS, CHUNK_STEPS[c] * STEP_ROWS
+            t = keep.tile([P, n, I], U8, name="x_bytes_%d" % c, align_bytes=64)
+            nc.sync.dma_start(out=t[:], in_=x_rows[:, s0 : s0 + n, :])
+            x_tiles[c] = t
+
+        def load_me(c):
+            s0, n = chunk_start[c] * STEP_ROWS, CHUNK_STEPS[c] * STEP_ROWS
+            t = keep.tile([P, n, OH], BF16, name="me_%d" % c, align_bytes=64)
+            nc.sync.dma_start(out=t[:], in_=me_rows[:, s0 : s0 + n, :])
+            me_tiles[c] = t
+
+        wi_raw = keep.tile([P, 4, OH], BF16, align_bytes=64)
+        wh_raw = keep.tile([P, 4, OH], BF16, align_bytes=64)
+        wt_raw = keep.tile([P, 4, H], BF16, align_bytes=64)
+        scale = keep.tile([P, 4], F32, align_bytes=64)
+        bias = keep.tile([P, 4], BF16, align_bytes=64)
+        load_x(0)
+        load_me(0)
+        nc.sync.dma_start(out=scale[:], in_=x_scale.rearrange("o (p t) -> p (o t)", p=P))
+        nc.sync.dma_start(out=wi_raw[:], in_=W_memi.rearrange("(p j) c -> p j c", j=4))
+        nc.sync.dma_start(out=wh_raw[:], in_=W_memh.rearrange("(p j) c -> p j c", j=4))
+        nc.sync.dma_start(out=bias[:], in_=mem_bias.rearrange("(p t) -> p t", t=4))
+        load_x(1)
+        load_me(1)
+        nc.sync.dma_start(out=wt_raw[:], in_=W_memt.rearrange("(p j) c -> p j c", j=4))
+        for c in range(2, FIRST_CHUNKS):
+            load_x(c)
+            load_me(c)
+
+        warm = keep.tile([P, 1], F32, align_bytes=64)
+        nc.vector.memset(warm[:], 0.0)
+        nc.scalar.activation(out=warm[:], in_=warm[:], func=SIGMOID)
+        ident = keep.tile([P, P], F32, align_bytes=64)
+        make_identity(nc, ident[:])
+
+        wi_g = keep.tile([P, 4 * OH], BF16, align_bytes=64)
+        wh_g0 = keep.tile([P, 2 * OH], BF16, align_bytes=64)
+        wh_g1 = keep.tile([P, 2 * OH], BF16, align_bytes=64)
+        wt_g = keep.tile([P, 4 * H], BF16, align_bytes=64)
+        wi_q = keep.tile([P, OH], U32, align_bytes=64)
+        wi_s = keep.tile([P, OH], U8, align_bytes=64)
+        wh_q = keep.tile([P, OH], U32, align_bytes=64)
+        wh_s = keep.tile([P, OH], U8, align_bytes=64)
+        wt_q = keep.tile([P, H], U32, align_bytes=64)
+        wt_s = keep.tile([P, H], U8, align_bytes=64)
+
+        def permuted(raw, t0, t1):
+            return raw[:].rearrange("p j (m t) -> p t m j", t=4)[:, t0:t1]
+
+        def grouped(g, nt):
+            return g[:].rearrange("p (t m j) -> p t m j", t=nt, j=4)
+
+        def quantize(q, s, g):
+            nc.vector.quantize_mx(out=q.bitcast(FP8X4), scales=s, in_=g)
+
+        xb, xg, mg, xq, xs, mq, ms = {}, {}, {}, {}, {}, {}, {}
+        bx, bm, ba, bb, bo, sig, gv, gg = {}, {}, {}, {}, {}, {}, {}, {}
+        gq, gs = {}, {}
+
+        def on(s):
+            return 0 <= s < STEPS
+
+        def widen(s):
+            c = chunk_of[s]
+            r0 = (s - chunk_start[c]) * STEP_ROWS
+            t = work.tile([P, STEP_ROWS * I], BF16, name="xb", align_bytes=64)
+            nc.scalar.copy(
+                out=t[:],
+                in_=x_tiles[c][:, r0 : r0 + STEP_ROWS, :].rearrange("p r k -> p (r k)").bitcast(FP8),
+            )
+            xb[s] = t
+
+        def transposes(bank, words):
+            for a in range(STEP_ROWS):
+                for u in range(2):
+                    nc.tensor.transpose(
+                        bank[:, u, a * P : (a + 1) * P], words[:, a * 256 + u : (a + 1) * 256 : 2], ident[:]
+                    )
+
+        def transpose_x(s):
+            t = psum.tile([P, 2, N], F32, name="bank_x", bufs=2)
+            transposes(t, xb.pop(s)[:].bitcast(F32))
+            bx[s] = t
+
+        def transpose_me(s):
+            c = chunk_of[s]
+            r0 = (s - chunk_start[c]) * STEP_ROWS
+            t = psum.tile([P, 2, N], F32, name="bank_m", bufs=2)
+            transposes(t, me_tiles[c][:, r0 : r0 + STEP_ROWS, :].rearrange("p r k -> p (r k)").bitcast(F32))
+            bm[s] = t
+
+        def scale_x(s):
+            t = work.tile([P, 4 * N], BF16, name="xg", bufs=3, align_bytes=64)
+            nc.vector.tensor_tensor(
+                out=t[:].rearrange("p (r u e) -> p r u e", u=2, e=2),
+                in0=bx.pop(s)[:].bitcast(BF16).rearrange("p u (r e) -> p r u e", e=2),
+                in1=scale[:].rearrange("p (u e) -> p u e", u=2).unsqueeze(1).broadcast_to([P, N, 2, 2]),
+                op=MULT,
+            )
+            xg[s] = t
+
+        def copy_me(s):
+            t = work.tile([P, 4 * N], BF16, name="mg", bufs=6, align_bytes=64)
+            nc.scalar.copy(
+                out=t[:].bitcast(F32).rearrange("p (r u) -> p r u", u=2),
+                in_=bm.pop(s)[:].rearrange("p u r -> p r u"),
+            )
+            mg[s] = t
+
+        def quantize_x(s):
+            xq[s] = work.tile([P, N], U32, name="xq", align_bytes=64)
+            xs[s] = work.tile([P, N], U8, name="xs", align_bytes=64)
+            quantize(xq[s][:], xs[s][:], xg.pop(s)[:])
+
+        def quantize_me(s):
+            mq[s] = work.tile([P, N], U32, name="mq", align_bytes=64)
+            ms[s] = work.tile([P, N], U8, name="ms", align_bytes=64)
+            quantize(mq[s][:], ms[s][:], mg[s][:])
+
+        def matmul1(s):
+            ba[s] = psum.tile([P, 2, N], F32, name="bank_a", bufs=1)
+            bb[s] = psum.tile([P, 2, N], F32, name="bank_b", bufs=1)
+            for t in range(4):
+                dst = (ba, bb)[t // 2][s][:, t % 2, :]
+                cols = slice(t * P, (t + 1) * P)
+                nc.tensor.matmul_mx(
+                    out=dst,
+                    lhsT=wi_q[:, cols].bitcast(FP8X4),
+                    lhsT_scale=wi_s[:, cols],
+                    rhs=xq[s][:].bitcast(FP8X4),
+                    rhs_scale=xs[s][:],
+                    start=True,
+                    stop=False,
+                )
+                nc.tensor.matmul_mx(
+                    out=dst,
+                    lhsT=wh_q[:, cols].bitcast(FP8X4),
+                    lhsT_scale=wh_s[:, cols],
+                    rhs=mq[s][:].bitcast(FP8X4),
+                    rhs_scale=ms[s][:],
+                    start=False,
+                    stop=True,
+                )
+
+        def sigmoids(s):
+            sig[s] = work.tile([P, 4, N], F32, name="sig", align_bytes=64)
+            for t in range(4):
+                nc.scalar.activation(
+                    out=sig[s][:, t, :], in_=(ba, bb)[t // 2][s][:, t % 2, :], func=SIGMOID, bias=bias[:, t : t + 1]
+                )
+
+        def gate(engine, dst, s, a):
+            engine.tensor_tensor(
+                out=dst[:].rearrange("p (c i t) -> p c t i", i=4, t=4),
+                in0=sig[s][:, :, a * P : (a + 1) * P].rearrange("p t (c i) -> p c t i", i=4),
+                in1=mg[s][:, a * P * 4 : (a + 1) * P * 4].rearrange("p (c i t) -> p c t i", i=4, t=4),
+                op=MULT,
+            )
+
+        def gate_v(s):
+            gv[s] = work.tile([P, 4 * P], BF16, name="gv", bufs=2, align_bytes=64)
+            gate(nc.vector, gv[s], s, 0)
+
+        def gate_g(s):
+            gg[s] = work.tile([P, 4 * P], BF16, name="gg", bufs=1, align_bytes=64)
+            gate(nc.gpsimd, gg[s], s, 1)
+
+        def quantize_gated(src, s, a):
+            gq[s, a] = work.tile([P, P], U32, name="gq%d" % a, align_bytes=64)
+            gs[s, a] = work.tile([P, P], U8, name="gs%d" % a, align_bytes=64)
+            quantize(gq[s, a][:], gs[s, a][:], src.pop(s)[:])
+
+        def matmul2(s):
+            bo[s] = psum.tile([P, 2, H], F32, name="bank_o", bufs=2)
+            for a in range(2):
+                nc.tensor.matmul_mx(
+                    out=bo[s][:, a, :],
+                    lhsT=gq[s, a][:].bitcast(FP8X4),
+                    lhsT_scale=gs[s, a][:],
+                    rhs=wt_q[:].bitcast(FP8X4),
+                    rhs_scale=wt_s[:],
+                    start=True,
+                    stop=True,
+                )
+
+        def store(s):
+            t = work.tile([P, STEP_ROWS, H], F32, name="result", bufs=4, align_bytes=64)
+            nc.scalar.copy(out=t[:], in_=bo.pop(s)[:])
+            nc.sync.dma_start(out=out_rows[:, s * STEP_ROWS : (s + 1) * STEP_ROWS, :], in_=t[:])
+
+        next_chunk = FIRST_CHUNKS
+        for j in range(-4, STEPS + 2):
+            while next_chunk < len(CHUNK_STEPS) and chunk_start[next_chunk] <= j + LOAD_LEAD:
+                load_x(next_chunk)
+                load_me(next_chunk)
+                next_chunk += 1
+            if j == -1:
+                nc.scalar.copy(out=grouped(wh_g1, 2), in_=permuted(wh_raw, 2, 4))
+                nc.vector.tensor_copy(out=grouped(wi_g, 4), in_=permuted(wi_raw, 0, 4))
+                nc.vector.tensor_copy(out=grouped(wh_g0, 2), in_=permuted(wh_raw, 0, 2))
+                quantize(wi_q[:], wi_s[:], wi_g[:])
+                quantize(wh_q[:, 0:256], wh_s[:, 0:256], wh_g0[:])
+                quantize(wh_q[:, 256:512], wh_s[:, 256:512], wh_g1[:])
+            if on(j - 1):
+                quantize_gated(gg, j - 1, 1)
+            if on(j + 2):
+                scale_x(j + 2)
+            if on(j):
+                gate_g(j)
+                gate_v(j)
+            if on(j + 2):
+                quantize_me(j + 2)
+                quantize_x(j + 2)
+            if on(j):
+                quantize_gated(gv, j, 0)
+            if j == 0:
+                nc.vector.tensor_copy(
+                    out=wt_g[:].rearrange("p (n j) -> p n j", j=4), in_=wt_raw[:].rearrange("p j n -> p n j")
+                )
+                quantize(wt_q[:], wt_s[:], wt_g[:])
+            if on(j + 1):
+                matmul1(j + 1)
+            if on(j + 3):
+                transpose_me(j + 3)
+                transpose_x(j + 3)
+            if on(j - 1):
+                matmul2(j - 1)
+            if on(j + 4):
+                widen(j + 4)
+            if on(j + 1):
+                sigmoids(j + 1)
+            if on(j - 1):
+                store(j - 1)
+            if on(j + 3):
+                copy_me(j + 3)

@@ -23,6 +23,7 @@ N = STEP_ROWS * P
 CHUNK_STEPS = [1, 1, 2] + [4] * 7
 FIRST_CHUNKS = 4
 LOAD_LEAD = 10
+V_WIDEN = 384
 
 
 def tile_lstmcell_pa_t_kernel(tc, x_bytes, x_scale, me_output, W_memi, W_memh, W_memt, mem_bias, out):
@@ -101,22 +102,23 @@ def tile_lstmcell_pa_t_kernel(tc, x_bytes, x_scale, me_output, W_memi, W_memh, W
         def quantize(q, s, g):
             nc.vector.quantize_mx(out=q.bitcast(FP8X4), scales=s, in_=g)
 
-        xb, xg, mg, xq, xs, mq, ms = {}, {}, {}, {}, {}, {}, {}
-        bx, bm, ba, bb, bo, sig, gv, gg = {}, {}, {}, {}, {}, {}, {}, {}
-        gq, gs = {}, {}
+        xb, xm, xmq, xms = {}, {}, {}, {}
+        bx, bm, ba, bb, bo, sig, gated, gq, gs = {}, {}, {}, {}, {}, {}, {}, {}, {}
 
         def on(s):
             return 0 <= s < STEPS
 
-        def widen(s):
+        def widen(engine, s):
             c = chunk_of[s]
             r0 = (s - chunk_start[c]) * STEP_ROWS
-            t = work.tile([P, STEP_ROWS * I], BF16, name="xb", align_bytes=64)
-            nc.scalar.copy(
-                out=t[:],
-                in_=x_tiles[c][:, r0 : r0 + STEP_ROWS, :].rearrange("p r k -> p (r k)").bitcast(FP8),
-            )
-            xb[s] = t
+            if s not in xb:
+                xb[s] = work.tile([P, STEP_ROWS * I], BF16, name="xb", align_bytes=64)
+            split = STEP_ROWS * I if s == 0 else V_WIDEN
+            codes = x_tiles[c][:, r0 : r0 + STEP_ROWS, :].rearrange("p r k -> p (r k)").bitcast(FP8)
+            if engine == "vector":
+                nc.vector.tensor_copy(out=xb[s][:, 0:split], in_=codes[:, 0:split])
+            elif split < STEP_ROWS * I:
+                nc.scalar.copy(out=xb[s][:, split:], in_=codes[:, split:])
 
         def transposes(bank, words):
             for a in range(STEP_ROWS):
@@ -138,32 +140,24 @@ def tile_lstmcell_pa_t_kernel(tc, x_bytes, x_scale, me_output, W_memi, W_memh, W
             bm[s] = t
 
         def scale_x(s):
-            t = work.tile([P, 4 * N], BF16, name="xg", bufs=3, align_bytes=64)
             nc.vector.tensor_tensor(
-                out=t[:].rearrange("p (r u e) -> p r u e", u=2, e=2),
+                out=xm[s][:, 0 : 4 * N].rearrange("p (r u e) -> p r u e", u=2, e=2),
                 in0=bx.pop(s)[:].bitcast(BF16).rearrange("p u (r e) -> p r u e", e=2),
                 in1=scale[:].rearrange("p (u e) -> p u e", u=2).unsqueeze(1).broadcast_to([P, N, 2, 2]),
                 op=MULT,
             )
-            xg[s] = t
 
         def copy_me(s):
-            t = work.tile([P, 4 * N], BF16, name="mg", bufs=6, align_bytes=64)
+            xm[s] = work.tile([P, 8 * N], BF16, name="xm", bufs=6, align_bytes=64)
             nc.scalar.copy(
-                out=t[:].bitcast(F32).rearrange("p (r u) -> p r u", u=2),
+                out=xm[s][:, 4 * N :].bitcast(F32).rearrange("p (r u) -> p r u", u=2),
                 in_=bm.pop(s)[:].rearrange("p u r -> p r u"),
             )
-            mg[s] = t
 
-        def quantize_x(s):
-            xq[s] = work.tile([P, N], U32, name="xq", align_bytes=64)
-            xs[s] = work.tile([P, N], U8, name="xs", align_bytes=64)
-            quantize(xq[s][:], xs[s][:], xg.pop(s)[:])
-
-        def quantize_me(s):
-            mq[s] = work.tile([P, N], U32, name="mq", align_bytes=64)
-            ms[s] = work.tile([P, N], U8, name="ms", align_bytes=64)
-            quantize(mq[s][:], ms[s][:], mg[s][:])
+        def quantize_xm(s):
+            xmq[s] = work.tile([P, 2 * N], U32, name="xmq", align_bytes=64)
+            xms[s] = work.tile([P, 2 * N], U8, name="xms", align_bytes=64)
+            quantize(xmq[s][:], xms[s][:], xm[s][:])
 
         def matmul1(s):
             ba[s] = psum.tile([P, 2, N], F32, name="bank_a", bufs=1)
@@ -175,8 +169,8 @@ def tile_lstmcell_pa_t_kernel(tc, x_bytes, x_scale, me_output, W_memi, W_memh, W
                     out=dst,
                     lhsT=wi_q[:, cols].bitcast(FP8X4),
                     lhsT_scale=wi_s[:, cols],
-                    rhs=xq[s][:].bitcast(FP8X4),
-                    rhs_scale=xs[s][:],
+                    rhs=xmq[s][:, 0:N].bitcast(FP8X4),
+                    rhs_scale=xms[s][:, 0:N],
                     start=True,
                     stop=False,
                 )
@@ -184,8 +178,8 @@ def tile_lstmcell_pa_t_kernel(tc, x_bytes, x_scale, me_output, W_memi, W_memh, W
                     out=dst,
                     lhsT=wh_q[:, cols].bitcast(FP8X4),
                     lhsT_scale=wh_s[:, cols],
-                    rhs=mq[s][:].bitcast(FP8X4),
-                    rhs_scale=ms[s][:],
+                    rhs=xmq[s][:, N:].bitcast(FP8X4),
+                    rhs_scale=xms[s][:, N:],
                     start=False,
                     stop=True,
                 )
@@ -197,34 +191,29 @@ def tile_lstmcell_pa_t_kernel(tc, x_bytes, x_scale, me_output, W_memi, W_memh, W
                     out=sig[s][:, t, :], in_=(ba, bb)[t // 2][s][:, t % 2, :], func=SIGMOID, bias=bias[:, t : t + 1]
                 )
 
-        def gate(engine, dst, s, a):
+        def gate(engine, s, a):
+            if s not in gated:
+                gated[s] = work.tile([P, 4 * N], BF16, name="gated", bufs=1, align_bytes=64)
+            cols = slice(a * P * 4, (a + 1) * P * 4)
             engine.tensor_tensor(
-                out=dst[:].rearrange("p (c i t) -> p c t i", i=4, t=4),
+                out=gated[s][:, cols].rearrange("p (c i t) -> p c t i", i=4, t=4),
                 in0=sig[s][:, :, a * P : (a + 1) * P].rearrange("p t (c i) -> p c t i", i=4),
-                in1=mg[s][:, a * P * 4 : (a + 1) * P * 4].rearrange("p (c i t) -> p c t i", i=4, t=4),
+                in1=xm[s][:, 4 * N :][:, cols].rearrange("p (c i t) -> p c t i", i=4, t=4),
                 op=MULT,
             )
 
-        def gate_v(s):
-            gv[s] = work.tile([P, 4 * P], BF16, name="gv", bufs=2, align_bytes=64)
-            gate(nc.vector, gv[s], s, 0)
-
-        def gate_g(s):
-            gg[s] = work.tile([P, 4 * P], BF16, name="gg", bufs=1, align_bytes=64)
-            gate(nc.gpsimd, gg[s], s, 1)
-
-        def quantize_gated(src, s, a):
-            gq[s, a] = work.tile([P, P], U32, name="gq%d" % a, align_bytes=64)
-            gs[s, a] = work.tile([P, P], U8, name="gs%d" % a, align_bytes=64)
-            quantize(gq[s, a][:], gs[s, a][:], src.pop(s)[:])
+        def quantize_gated(s):
+            gq[s] = work.tile([P, N], U32, name="gq", align_bytes=64)
+            gs[s] = work.tile([P, N], U8, name="gs", align_bytes=64)
+            quantize(gq[s][:], gs[s][:], gated[s][:])
 
         def matmul2(s):
             bo[s] = psum.tile([P, 2, H], F32, name="bank_o", bufs=2)
             for a in range(2):
                 nc.tensor.matmul_mx(
                     out=bo[s][:, a, :],
-                    lhsT=gq[s, a][:].bitcast(FP8X4),
-                    lhsT_scale=gs[s, a][:],
+                    lhsT=gq[s][:, a * P : (a + 1) * P].bitcast(FP8X4),
+                    lhsT_scale=gs[s][:, a * P : (a + 1) * P],
                     rhs=wt_q[:].bitcast(FP8X4),
                     rhs_scale=wt_s[:],
                     start=True,
@@ -250,17 +239,16 @@ def tile_lstmcell_pa_t_kernel(tc, x_bytes, x_scale, me_output, W_memi, W_memh, W
                 quantize(wh_q[:, 0:256], wh_s[:, 0:256], wh_g0[:])
                 quantize(wh_q[:, 256:512], wh_s[:, 256:512], wh_g1[:])
             if on(j - 1):
-                quantize_gated(gg, j - 1, 1)
+                quantize_gated(j - 1)
             if on(j + 2):
                 scale_x(j + 2)
             if on(j):
-                gate_g(j)
-                gate_v(j)
+                gate(nc.gpsimd, j, 1)
+                gate(nc.vector, j, 0)
+            if on(j + 4):
+                widen("vector", j + 4)
             if on(j + 2):
-                quantize_me(j + 2)
-                quantize_x(j + 2)
-            if on(j):
-                quantize_gated(gv, j, 0)
+                quantize_xm(j + 2)
             if j == 0:
                 nc.vector.tensor_copy(
                     out=wt_g[:].rearrange("p (n j) -> p n j", j=4), in_=wt_raw[:].rearrange("p j n -> p n j")
@@ -274,7 +262,7 @@ def tile_lstmcell_pa_t_kernel(tc, x_bytes, x_scale, me_output, W_memi, W_memh, W
             if on(j - 1):
                 matmul2(j - 1)
             if on(j + 4):
-                widen(j + 4)
+                widen("scalar", j + 4)
             if on(j + 1):
                 sigmoids(j + 1)
             if on(j - 1):

@@ -23,7 +23,6 @@ N = STEP_ROWS * P
 CHUNK_STEPS = [1, 1, 2] + [4] * 7
 FIRST_CHUNKS = 4
 LOAD_LEAD = 10
-V_WIDEN = 384
 
 
 def tile_lstmcell_pa_t_kernel(tc, x_bytes, x_scale, me_output, W_memi, W_memh, W_memt, mem_bias, out):
@@ -63,9 +62,9 @@ def tile_lstmcell_pa_t_kernel(tc, x_bytes, x_scale, me_output, W_memi, W_memh, W
         wt_raw = keep.tile([P, 4, H], BF16, align_bytes=64)
         scale = keep.tile([P, 4], F32, align_bytes=64)
         bias = keep.tile([P, 4], BF16, align_bytes=64)
+        nc.sync.dma_start(out=scale[:], in_=x_scale.rearrange("o (p t) -> p (o t)", p=P))
         load_x(0)
         load_me(0)
-        nc.sync.dma_start(out=scale[:], in_=x_scale.rearrange("o (p t) -> p (o t)", p=P))
         nc.sync.dma_start(out=wi_raw[:], in_=W_memi.rearrange("(p j) c -> p j c", j=4))
         nc.sync.dma_start(out=wh_raw[:], in_=W_memh.rearrange("(p j) c -> p j c", j=4))
         nc.sync.dma_start(out=bias[:], in_=mem_bias.rearrange("(p t) -> p t", t=4))
@@ -81,6 +80,18 @@ def tile_lstmcell_pa_t_kernel(tc, x_bytes, x_scale, me_output, W_memi, W_memh, W
         nc.scalar.activation(out=warm[:], in_=warm[:], func=SIGMOID)
         ident = keep.tile([P, P], F32, align_bytes=64)
         make_identity(nc, ident[:])
+
+        bank_s = psum.tile([P, 2, N], F32, name="bank_x", bufs=2)
+        for t in range(4):
+            nc.tensor.transpose(
+                bank_s[:, t // 2, (t % 2) * P : (t % 2 + 1) * P], scale[:, t : t + 1].to_broadcast([P, P]), ident[:]
+            )
+        scale_row = keep.tile([P, STEP_ROWS * I], F32, align_bytes=64)
+        for a in range(STEP_ROWS):
+            nc.scalar.copy(
+                out=scale_row[:, a * I : (a + 1) * I].rearrange("p (n h t) -> p n h t", h=2, t=2),
+                in_=bank_s[:].rearrange("p h (t n) -> p n h t", t=2),
+            )
 
         wi_g = keep.tile([P, 4 * OH], BF16, align_bytes=64)
         wh_g0 = keep.tile([P, 2 * OH], BF16, align_bytes=64)
@@ -108,17 +119,16 @@ def tile_lstmcell_pa_t_kernel(tc, x_bytes, x_scale, me_output, W_memi, W_memh, W
         def on(s):
             return 0 <= s < STEPS
 
-        def widen(engine, s):
+        def product_x(s):
             c = chunk_of[s]
             r0 = (s - chunk_start[c]) * STEP_ROWS
-            if s not in xb:
-                xb[s] = work.tile([P, STEP_ROWS * I], BF16, name="xb", align_bytes=64)
-            split = STEP_ROWS * I if s == 0 else V_WIDEN
-            codes = x_tiles[c][:, r0 : r0 + STEP_ROWS, :].rearrange("p r k -> p (r k)").bitcast(FP8)
-            if engine == "vector":
-                nc.vector.tensor_copy(out=xb[s][:, 0:split], in_=codes[:, 0:split])
-            elif split < STEP_ROWS * I:
-                nc.scalar.copy(out=xb[s][:, split:], in_=codes[:, split:])
+            xb[s] = work.tile([P, STEP_ROWS * I], BF16, name="xb", align_bytes=64)
+            nc.vector.tensor_tensor(
+                out=xb[s][:],
+                in0=x_tiles[c][:, r0 : r0 + STEP_ROWS, :].rearrange("p r k -> p (r k)").bitcast(FP8),
+                in1=scale_row[:],
+                op=MULT,
+            )
 
         def transposes(bank, words):
             for a in range(STEP_ROWS):
@@ -139,20 +149,17 @@ def tile_lstmcell_pa_t_kernel(tc, x_bytes, x_scale, me_output, W_memi, W_memh, W
             transposes(t, me_tiles[c][:, r0 : r0 + STEP_ROWS, :].rearrange("p r k -> p (r k)").bitcast(F32))
             bm[s] = t
 
-        def scale_x(s):
-            nc.vector.tensor_tensor(
-                out=xm[s][:, 0 : 4 * N].rearrange("p (r u e) -> p r u e", u=2, e=2),
-                in0=bx.pop(s)[:].bitcast(BF16).rearrange("p u (r e) -> p r u e", e=2),
-                in1=scale[:].rearrange("p (u e) -> p u e", u=2).unsqueeze(1).broadcast_to([P, N, 2, 2]),
-                op=MULT,
+        def copy_out(bank, dst):
+            nc.scalar.copy(
+                out=dst.bitcast(F32).rearrange("p (r u) -> p r u", u=2), in_=bank[:].rearrange("p u r -> p r u")
             )
 
         def copy_me(s):
             xm[s] = work.tile([P, 8 * N], BF16, name="xm", bufs=6, align_bytes=64)
-            nc.scalar.copy(
-                out=xm[s][:, 4 * N :].bitcast(F32).rearrange("p (r u) -> p r u", u=2),
-                in_=bm.pop(s)[:].rearrange("p u r -> p r u"),
-            )
+            copy_out(bm.pop(s), xm[s][:, 4 * N :])
+
+        def copy_x(s):
+            copy_out(bx.pop(s), xm[s][:, 0 : 4 * N])
 
         def quantize_xm(s):
             xmq[s] = work.tile([P, 2 * N], U32, name="xmq", align_bytes=64)
@@ -191,14 +198,12 @@ def tile_lstmcell_pa_t_kernel(tc, x_bytes, x_scale, me_output, W_memi, W_memh, W
                     out=sig[s][:, t, :], in_=(ba, bb)[t // 2][s][:, t % 2, :], func=SIGMOID, bias=bias[:, t : t + 1]
                 )
 
-        def gate(engine, s, a):
-            if s not in gated:
-                gated[s] = work.tile([P, 4 * N], BF16, name="gated", bufs=1, align_bytes=64)
-            cols = slice(a * P * 4, (a + 1) * P * 4)
-            engine.tensor_tensor(
-                out=gated[s][:, cols].rearrange("p (c i t) -> p c t i", i=4, t=4),
-                in0=sig[s][:, :, a * P : (a + 1) * P].rearrange("p t (c i) -> p c t i", i=4),
-                in1=xm[s][:, 4 * N :][:, cols].rearrange("p (c i t) -> p c t i", i=4, t=4),
+        def gate(s):
+            gated[s] = work.tile([P, 4 * N], BF16, name="gated", bufs=2, align_bytes=64)
+            nc.vector.tensor_tensor(
+                out=gated[s][:].rearrange("p (c i t) -> p c t i", i=4, t=4),
+                in0=sig[s][:].rearrange("p t (c i) -> p c t i", i=4),
+                in1=xm[s][:, 4 * N :].rearrange("p (c i t) -> p c t i", i=4, t=4),
                 op=MULT,
             )
 
@@ -240,13 +245,10 @@ def tile_lstmcell_pa_t_kernel(tc, x_bytes, x_scale, me_output, W_memi, W_memh, W
                 quantize(wh_q[:, 256:512], wh_s[:, 256:512], wh_g1[:])
             if on(j - 1):
                 quantize_gated(j - 1)
-            if on(j + 2):
-                scale_x(j + 2)
-            if on(j):
-                gate(nc.gpsimd, j, 1)
-                gate(nc.vector, j, 0)
             if on(j + 4):
-                widen("vector", j + 4)
+                product_x(j + 4)
+            if on(j):
+                gate(j)
             if on(j + 2):
                 quantize_xm(j + 2)
             if j == 0:
@@ -261,11 +263,10 @@ def tile_lstmcell_pa_t_kernel(tc, x_bytes, x_scale, me_output, W_memi, W_memh, W
                 transpose_x(j + 3)
             if on(j - 1):
                 matmul2(j - 1)
-            if on(j + 4):
-                widen("scalar", j + 4)
             if on(j + 1):
                 sigmoids(j + 1)
             if on(j - 1):
                 store(j - 1)
             if on(j + 3):
                 copy_me(j + 3)
+                copy_x(j + 3)

@@ -20,7 +20,8 @@ ROWS = B // P
 STEP_ROWS = 2
 STEPS = ROWS // STEP_ROWS
 N = STEP_ROWS * P
-CHUNK_STEPS = [1, 1, 2] + [4] * 7
+GROUPS = [1, 1] + [2] * 14 + [1, 1]
+CHUNKS = [1, 1, 2] + [4] * 7
 FIRST_CHUNKS = 4
 LOAD_LEAD = 10
 
@@ -30,6 +31,10 @@ def tile_lstmcell_pa_t_kernel(tc, x_bytes, x_scale, me_output, W_memi, W_memh, W
     x_rows = x_bytes.rearrange("(p r) k -> p r k", p=P)
     me_rows = me_output.rearrange("(p r) k -> p r k", p=P)
     out_rows = out.rearrange("(p r) n -> p r n", p=P)
+    group_start = [sum(GROUPS[:g]) for g in range(len(GROUPS))]
+    group_of = [g for g, n in enumerate(GROUPS) for i in range(n)]
+    chunk_start = [sum(CHUNKS[:c]) for c in range(len(CHUNKS))]
+    chunk_of = [c for c, n in enumerate(CHUNKS) for i in range(n)]
 
     with ExitStack() as ctx:
         keep = ctx.enter_context(tc.tile_pool(name="keep", bufs=1))
@@ -37,25 +42,21 @@ def tile_lstmcell_pa_t_kernel(tc, x_bytes, x_scale, me_output, W_memi, W_memh, W
         psum = ctx.enter_context(tc.psum_pool(name="psum", bufs=1))
         ctx.enter_context(tc.manual_schedule())
 
-        chunk_of = []
-        chunk_start = []
-        for c, n in enumerate(CHUNK_STEPS):
-            chunk_start.append(len(chunk_of))
-            chunk_of.extend([c] * n)
-        x_tiles = {}
-        me_tiles = {}
+        x_in, me_in = {}, {}
 
         def load_x(c):
-            s0, n = chunk_start[c] * STEP_ROWS, CHUNK_STEPS[c] * STEP_ROWS
-            t = keep.tile([P, n, I], U8, name="x_bytes_%d" % c, align_bytes=64)
-            nc.sync.dma_start(out=t[:], in_=x_rows[:, s0 : s0 + n, :])
-            x_tiles[c] = t
+            r0, n = chunk_start[c] * STEP_ROWS, CHUNKS[c] * STEP_ROWS
+            x_in[c] = work.tile([P, n * I], U8, name="x_in", bufs=4, align_bytes=64)
+            nc.sync.dma_start(
+                out=x_in[c][:].rearrange("p (r k) -> p r k", k=I), in_=x_rows[:, r0 : r0 + n, :]
+            )
 
         def load_me(c):
-            s0, n = chunk_start[c] * STEP_ROWS, CHUNK_STEPS[c] * STEP_ROWS
-            t = keep.tile([P, n, OH], BF16, name="me_%d" % c, align_bytes=64)
-            nc.sync.dma_start(out=t[:], in_=me_rows[:, s0 : s0 + n, :])
-            me_tiles[c] = t
+            r0, n = chunk_start[c] * STEP_ROWS, CHUNKS[c] * STEP_ROWS
+            me_in[c] = work.tile([P, n * OH], BF16, name="me_in", bufs=4, align_bytes=64)
+            nc.sync.dma_start(
+                out=me_in[c][:].rearrange("p (r k) -> p r k", k=OH), in_=me_rows[:, r0 : r0 + n, :]
+            )
 
         wi_raw = keep.tile([P, 4, OH], BF16, align_bytes=64)
         wh_raw = keep.tile([P, 4, OH], BF16, align_bytes=64)
@@ -65,15 +66,16 @@ def tile_lstmcell_pa_t_kernel(tc, x_bytes, x_scale, me_output, W_memi, W_memh, W
         nc.sync.dma_start(out=scale[:], in_=x_scale.rearrange("o (p t) -> p (o t)", p=P))
         load_x(0)
         load_me(0)
+        load_x(1)
         nc.sync.dma_start(out=wi_raw[:], in_=W_memi.rearrange("(p j) c -> p j c", j=4))
         nc.sync.dma_start(out=wh_raw[:], in_=W_memh.rearrange("(p j) c -> p j c", j=4))
         nc.sync.dma_start(out=bias[:], in_=mem_bias.rearrange("(p t) -> p t", t=4))
-        load_x(1)
         load_me(1)
+        load_x(2)
+        load_me(2)
         nc.sync.dma_start(out=wt_raw[:], in_=W_memt.rearrange("(p j) c -> p j c", j=4))
-        for c in range(2, FIRST_CHUNKS):
-            load_x(c)
-            load_me(c)
+        load_x(3)
+        load_me(3)
 
         warm = keep.tile([P, 1], F32, align_bytes=64)
         nc.vector.memset(warm[:], 0.0)
@@ -81,21 +83,20 @@ def tile_lstmcell_pa_t_kernel(tc, x_bytes, x_scale, me_output, W_memi, W_memh, W
         ident = keep.tile([P, P], F32, align_bytes=64)
         make_identity(nc, ident[:])
 
+        scale_row = keep.tile([P, max(GROUPS) * STEP_ROWS * I], F32, align_bytes=64)
         bank_s = psum.tile([P, 2, N], F32, name="bank_x", bufs=2)
         for t in range(4):
             nc.tensor.transpose(
                 bank_s[:, t // 2, (t % 2) * P : (t % 2 + 1) * P], scale[:, t : t + 1].to_broadcast([P, P]), ident[:]
             )
-        scale_row = keep.tile([P, STEP_ROWS * I], F32, align_bytes=64)
-        for a in range(STEP_ROWS):
-            nc.scalar.copy(
-                out=scale_row[:, a * I : (a + 1) * I].rearrange("p (n h t) -> p n h t", h=2, t=2),
-                in_=bank_s[:].rearrange("p h (t n) -> p n h t", t=2),
-            )
+        nc.scalar.copy(
+            out=scale_row[:, 0:I].rearrange("p (n h t) -> p n h t", h=2, t=2),
+            in_=bank_s[:].rearrange("p h (t n) -> p n h t", t=2),
+        )
+        nc.vector.tensor_copy(out=scale_row[:, I : 2 * I], in_=scale_row[:, 0:I])
 
         wi_g = keep.tile([P, 4 * OH], BF16, align_bytes=64)
-        wh_g0 = keep.tile([P, 2 * OH], BF16, align_bytes=64)
-        wh_g1 = keep.tile([P, 2 * OH], BF16, align_bytes=64)
+        wh_g = [keep.tile([P, 2 * OH], BF16, name="wh_g%d" % i, align_bytes=64) for i in range(2)]
         wt_g = keep.tile([P, 4 * H], BF16, align_bytes=64)
         wi_q = keep.tile([P, OH], U32, align_bytes=64)
         wi_s = keep.tile([P, OH], U8, align_bytes=64)
@@ -113,21 +114,22 @@ def tile_lstmcell_pa_t_kernel(tc, x_bytes, x_scale, me_output, W_memi, W_memh, W
         def quantize(q, s, g):
             nc.vector.quantize_mx(out=q.bitcast(FP8X4), scales=s, in_=g)
 
-        xb, xm, xmq, xms = {}, {}, {}, {}
-        bx, bm, ba, bb, bo, sig, gated, gq, gs = {}, {}, {}, {}, {}, {}, {}, {}, {}
+        xb, xm, xmq, xms, sig, gated, gq, gs = {}, {}, {}, {}, {}, {}, {}, {}
+        bx, bm, ba, bb, bo = {}, {}, {}, {}, {}
 
-        def on(s):
-            return 0 <= s < STEPS
+        def steps(g):
+            return range(group_start[g], group_start[g] + GROUPS[g]) if 0 <= g < len(GROUPS) else range(0)
 
-        def product_x(s):
-            c = chunk_of[s]
-            r0 = (s - chunk_start[c]) * STEP_ROWS
-            xb[s] = work.tile([P, STEP_ROWS * I], BF16, name="xb", align_bytes=64)
+        def place(s):
+            return group_of[s], s - group_start[group_of[s]]
+
+        def product_x(g):
+            n = GROUPS[g] * STEP_ROWS * I
+            c = chunk_of[group_start[g]]
+            c0 = (group_start[g] - chunk_start[c]) * STEP_ROWS * I
+            xb[g] = work.tile([P, n], BF16, name="xb", align_bytes=64)
             nc.vector.tensor_tensor(
-                out=xb[s][:],
-                in0=x_tiles[c][:, r0 : r0 + STEP_ROWS, :].rearrange("p r k -> p (r k)").bitcast(FP8),
-                in1=scale_row[:],
-                op=MULT,
+                out=xb[g][:], in0=x_in[c][:, c0 : c0 + n].bitcast(FP8), in1=scale_row[:, 0:n], op=MULT
             )
 
         def transposes(bank, words):
@@ -138,135 +140,170 @@ def tile_lstmcell_pa_t_kernel(tc, x_bytes, x_scale, me_output, W_memi, W_memh, W
                     )
 
         def transpose_x(s):
-            t = psum.tile([P, 2, N], F32, name="bank_x", bufs=2)
-            transposes(t, xb.pop(s)[:].bitcast(F32))
-            bx[s] = t
+            g, h = place(s)
+            bx[s] = psum.tile([P, 2, N], F32, name="bank_x", bufs=2)
+            transposes(bx[s], xb[g][:, h * 1024 : (h + 1) * 1024].bitcast(F32))
 
         def transpose_me(s):
             c = chunk_of[s]
-            r0 = (s - chunk_start[c]) * STEP_ROWS
-            t = psum.tile([P, 2, N], F32, name="bank_m", bufs=2)
-            transposes(t, me_tiles[c][:, r0 : r0 + STEP_ROWS, :].rearrange("p r k -> p (r k)").bitcast(F32))
-            bm[s] = t
+            c0 = (s - chunk_start[c]) * STEP_ROWS * OH
+            bm[s] = psum.tile([P, 2, N], F32, name="bank_m", bufs=2)
+            transposes(bm[s], me_in[c][:, c0 : c0 + STEP_ROWS * OH].bitcast(F32))
 
         def copy_out(bank, dst):
             nc.scalar.copy(
                 out=dst.bitcast(F32).rearrange("p (r u) -> p r u", u=2), in_=bank[:].rearrange("p u r -> p r u")
             )
 
+        def me_cols(g):
+            return GROUPS[g] * 4 * N
+
         def copy_me(s):
-            xm[s] = work.tile([P, 8 * N], BF16, name="xm", bufs=6, align_bytes=64)
-            copy_out(bm.pop(s), xm[s][:, 4 * N :])
+            g, h = place(s)
+            if h == 0:
+                xm[g] = work.tile([P, 2 * me_cols(g)], BF16, name="xm", bufs=5, align_bytes=64)
+            m0 = me_cols(g) + h * 4 * N
+            copy_out(bm.pop(s), xm[g][:, m0 : m0 + 4 * N])
 
         def copy_x(s):
-            copy_out(bx.pop(s), xm[s][:, 0 : 4 * N])
+            g, h = place(s)
+            copy_out(bx.pop(s), xm[g][:, h * 4 * N : (h + 1) * 4 * N])
 
-        def quantize_xm(s):
-            xmq[s] = work.tile([P, 2 * N], U32, name="xmq", align_bytes=64)
-            xms[s] = work.tile([P, 2 * N], U8, name="xms", align_bytes=64)
-            quantize(xmq[s][:], xms[s][:], xm[s][:])
+        def quantize_xm(g):
+            n = 2 * GROUPS[g] * N
+            xmq[g] = work.tile([P, n], U32, name="xmq", align_bytes=64)
+            xms[g] = work.tile([P, n], U8, name="xms", align_bytes=64)
+            quantize(xmq[g][:], xms[g][:], xm[g][:])
 
         def matmul1(s):
+            g, h = place(s)
             ba[s] = psum.tile([P, 2, N], F32, name="bank_a", bufs=1)
             bb[s] = psum.tile([P, 2, N], F32, name="bank_b", bufs=1)
             for t in range(4):
-                dst = (ba, bb)[t // 2][s][:, t % 2, :]
-                cols = slice(t * P, (t + 1) * P)
-                nc.tensor.matmul_mx(
-                    out=dst,
-                    lhsT=wi_q[:, cols].bitcast(FP8X4),
-                    lhsT_scale=wi_s[:, cols],
-                    rhs=xmq[s][:, 0:N].bitcast(FP8X4),
-                    rhs_scale=xms[s][:, 0:N],
-                    start=True,
-                    stop=False,
-                )
-                nc.tensor.matmul_mx(
-                    out=dst,
-                    lhsT=wh_q[:, cols].bitcast(FP8X4),
-                    lhsT_scale=wh_s[:, cols],
-                    rhs=xmq[s][:, N:].bitcast(FP8X4),
-                    rhs_scale=xms[s][:, N:],
-                    start=False,
-                    stop=True,
-                )
+                w = slice(t * P, (t + 1) * P)
+                for i in range(2):
+                    wq, ws = ((wi_q, wi_s), (wh_q, wh_s))[i]
+                    c0 = (i * GROUPS[g] + h) * N
+                    nc.tensor.matmul_mx(
+                        out=(ba, bb)[t // 2][s][:, t % 2, :],
+                        lhsT=wq[:, w].bitcast(FP8X4),
+                        lhsT_scale=ws[:, w],
+                        rhs=xmq[g][:, c0 : c0 + N].bitcast(FP8X4),
+                        rhs_scale=xms[g][:, c0 : c0 + N],
+                        start=(i == 0),
+                        stop=(i == 1),
+                    )
 
         def sigmoids(s):
-            sig[s] = work.tile([P, 4, N], F32, name="sig", align_bytes=64)
+            g, h = place(s)
+            if h == 0:
+                sig[g] = work.tile([P, 4, GROUPS[g] * N], F32, name="sig", align_bytes=64)
             for t in range(4):
                 nc.scalar.activation(
-                    out=sig[s][:, t, :], in_=(ba, bb)[t // 2][s][:, t % 2, :], func=SIGMOID, bias=bias[:, t : t + 1]
+                    out=sig[g][:, t, h * N : (h + 1) * N],
+                    in_=(ba, bb)[t // 2][s][:, t % 2, :],
+                    func=SIGMOID,
+                    bias=bias[:, t : t + 1],
                 )
 
-        def gate(s):
-            gated[s] = work.tile([P, 4 * N], BF16, name="gated", bufs=2, align_bytes=64)
+        def gate(g, n0, n1):
+            if n0 == 0:
+                gated[g] = work.tile([P, me_cols(g)], BF16, name="gated", bufs=2, align_bytes=64)
+            m0 = me_cols(g)
             nc.vector.tensor_tensor(
-                out=gated[s][:].rearrange("p (c i t) -> p c t i", i=4, t=4),
-                in0=sig[s][:].rearrange("p t (c i) -> p c t i", i=4),
-                in1=xm[s][:, 4 * N :].rearrange("p (c i t) -> p c t i", i=4, t=4),
+                out=gated[g][:, 4 * n0 : 4 * n1].rearrange("p (c i t) -> p c t i", i=4, t=4),
+                in0=sig[g][:, :, n0:n1].rearrange("p t (c i) -> p c t i", i=4),
+                in1=xm[g][:, m0 + 4 * n0 : m0 + 4 * n1].rearrange("p (c i t) -> p c t i", i=4, t=4),
                 op=MULT,
             )
 
-        def quantize_gated(s):
-            gq[s] = work.tile([P, N], U32, name="gq", align_bytes=64)
-            gs[s] = work.tile([P, N], U8, name="gs", align_bytes=64)
-            quantize(gq[s][:], gs[s][:], gated[s][:])
+        def quantize_gated(g, n0, n1):
+            if n0 == 0:
+                gq[g] = work.tile([P, GROUPS[g] * N], U32, name="gq", align_bytes=64)
+                gs[g] = work.tile([P, GROUPS[g] * N], U8, name="gs", align_bytes=64)
+            quantize(gq[g][:, n0:n1], gs[g][:, n0:n1], gated[g][:, 4 * n0 : 4 * n1])
+
+        def matmul2_row(bank_row, g, n0):
+            nc.tensor.matmul_mx(
+                out=bank_row,
+                lhsT=gq[g][:, n0 : n0 + P].bitcast(FP8X4),
+                lhsT_scale=gs[g][:, n0 : n0 + P],
+                rhs=wt_q[:].bitcast(FP8X4),
+                rhs_scale=wt_s[:],
+                start=True,
+                stop=True,
+            )
 
         def matmul2(s):
+            g, h = place(s)
             bo[s] = psum.tile([P, 2, H], F32, name="bank_o", bufs=2)
             for a in range(2):
-                nc.tensor.matmul_mx(
-                    out=bo[s][:, a, :],
-                    lhsT=gq[s][:, a * P : (a + 1) * P].bitcast(FP8X4),
-                    lhsT_scale=gs[s][:, a * P : (a + 1) * P],
-                    rhs=wt_q[:].bitcast(FP8X4),
-                    rhs_scale=wt_s[:],
-                    start=True,
-                    stop=True,
-                )
+                matmul2_row(bo[s][:, a, :], g, h * N + a * P)
 
         def store(s):
             t = work.tile([P, STEP_ROWS, H], F32, name="result", bufs=4, align_bytes=64)
             nc.scalar.copy(out=t[:], in_=bo.pop(s)[:])
             nc.sync.dma_start(out=out_rows[:, s * STEP_ROWS : (s + 1) * STEP_ROWS, :], in_=t[:])
 
+        last = len(GROUPS) - 1
         next_chunk = FIRST_CHUNKS
-        for j in range(-4, STEPS + 2):
-            while next_chunk < len(CHUNK_STEPS) and chunk_start[next_chunk] <= j + LOAD_LEAD:
+        for j in range(-4, last + 2):
+            reach = group_start[min(max(j, 0), last)]
+            while next_chunk < len(CHUNKS) and chunk_start[next_chunk] <= reach + LOAD_LEAD:
                 load_x(next_chunk)
                 load_me(next_chunk)
                 next_chunk += 1
-            if j == -1:
-                nc.scalar.copy(out=grouped(wh_g1, 2), in_=permuted(wh_raw, 2, 4))
-                nc.vector.tensor_copy(out=grouped(wi_g, 4), in_=permuted(wi_raw, 0, 4))
-                nc.vector.tensor_copy(out=grouped(wh_g0, 2), in_=permuted(wh_raw, 0, 2))
-                quantize(wi_q[:], wi_s[:], wi_g[:])
-                quantize(wh_q[:, 0:256], wh_s[:, 0:256], wh_g0[:])
-                quantize(wh_q[:, 256:512], wh_s[:, 256:512], wh_g1[:])
-            if on(j - 1):
-                quantize_gated(j - 1)
-            if on(j + 4):
+            ahead = 0 <= j + 4 <= last
+            if ahead and j != -2:
                 product_x(j + 4)
-            if on(j):
-                gate(j)
-            if on(j + 2):
+            if j == -3:
+                nc.vector.tensor_copy(out=grouped(wi_g, 4), in_=permuted(wi_raw, 0, 4))
+            if 0 <= j < last:
+                gate(j, 0, GROUPS[j] * N)
+            if 0 <= j + 2 <= last:
                 quantize_xm(j + 2)
+            if j == -2:
+                quantize(wi_q[:], wi_s[:], wi_g[:])
+                product_x(j + 4)
+                for i in range(2):
+                    quantize(wh_q[:, i * 256 : (i + 1) * 256], wh_s[:, i * 256 : (i + 1) * 256], wh_g[i][:])
+            if 0 <= j < last:
+                quantize_gated(j, 0, GROUPS[j] * N)
             if j == 0:
-                nc.vector.tensor_copy(
+                quantize(wt_q[:], wt_s[:], wt_g[:])
+            if j == last:
+                for a in range(2):
+                    gate(j, a * P, (a + 1) * P)
+                for a in range(2):
+                    quantize_gated(j, a * P, (a + 1) * P)
+                for a in range(2):
+                    bank = psum.tile([P, 2, H], F32, name="bank_o", bufs=2)
+                    matmul2_row(bank[:, 0, :], j, a * P)
+                    res = work.tile([P, H], F32, name="result_row", bufs=2, align_bytes=64)
+                    if a == 0:
+                        nc.scalar.copy(out=res[:], in_=bank[:, 0, :])
+                    else:
+                        nc.vector.tensor_copy(out=res[:], in_=bank[:, 0, :])
+                    nc.sync.dma_start(out=out_rows[:, ROWS - 2 + a, :], in_=res[:])
+            m1, t, m2 = list(steps(j + 1)), list(steps(j + 3)), list(steps(j - 1)) if j <= last else []
+            for h in range(2):
+                for s in m1[h : h + 1]:
+                    matmul1(s)
+                    sigmoids(s)
+                for s in m2[h : h + 1]:
+                    matmul2(s)
+                    store(s)
+                for s in t[h : h + 1]:
+                    transpose_me(s)
+                    copy_me(s)
+                    if j == -3:
+                        nc.scalar.copy(out=scale_row[:, 2 * I :], in_=scale_row[:, 0 : 2 * I])
+                        nc.scalar.copy(out=grouped(wh_g[0], 2), in_=permuted(wh_raw, 0, 2))
+                    transpose_x(s)
+                    copy_x(s)
+            if j == -3:
+                nc.scalar.copy(out=grouped(wh_g[1], 2), in_=permuted(wh_raw, 2, 4))
+            if j == -1:
+                nc.scalar.copy(
                     out=wt_g[:].rearrange("p (n j) -> p n j", j=4), in_=wt_raw[:].rearrange("p j n -> p n j")
                 )
-                quantize(wt_q[:], wt_s[:], wt_g[:])
-            if on(j + 1):
-                matmul1(j + 1)
-            if on(j + 3):
-                transpose_me(j + 3)
-                transpose_x(j + 3)
-            if on(j - 1):
-                matmul2(j - 1)
-            if on(j + 1):
-                sigmoids(j + 1)
-            if on(j - 1):
-                store(j - 1)
-            if on(j + 3):
-                copy_me(j + 3)
-                copy_x(j + 3)

@@ -197,11 +197,12 @@ def tile_lstmcell_pa_t_kernel(tc, x_bytes, x_scale, me_output, W_memi, W_memh, W
         def sigmoids(s):
             g, h = place(s)
             if h == 0:
-                sig[g] = work.tile([P, 4, GROUPS[g] * N], F32, name="sig", align_bytes=64)
+                sig[g] = work.tile([P, GROUPS[g] * 4 * N], F32, name="sig", align_bytes=64)
+            quads = sig[g][:, h * 4 * N : (h + 1) * 4 * N].rearrange("p (c t i) -> p c t i", t=4, i=4)
             for t in range(4):
                 nc.scalar.activation(
-                    out=sig[g][:, t, h * N : (h + 1) * N],
-                    in_=(ba, bb)[t // 2][s][:, t % 2, :],
+                    out=quads[:, :, t, :],
+                    in_=(ba, bb)[t // 2][s][:, t % 2, :].rearrange("p (c i) -> p c i", i=4),
                     func=SIGMOID,
                     bias=bias[:, t : t + 1],
                 )
@@ -212,7 +213,7 @@ def tile_lstmcell_pa_t_kernel(tc, x_bytes, x_scale, me_output, W_memi, W_memh, W
             m0 = me_cols(g)
             nc.vector.tensor_tensor(
                 out=gated[g][:, 4 * n0 : 4 * n1].rearrange("p (c i t) -> p c t i", i=4, t=4),
-                in0=sig[g][:, :, n0:n1].rearrange("p t (c i) -> p c t i", i=4),
+                in0=sig[g][:, 4 * n0 : 4 * n1].rearrange("p (c t i) -> p c t i", i=4, t=4),
                 in1=xm[g][:, m0 + 4 * n0 : m0 + 4 * n1].rearrange("p (c i t) -> p c t i", i=4, t=4),
                 op=MULT,
             )

from contextlib import ExitStack

import concourse.mybir as mybir
from concourse.masks import make_identity

B, I, H, OH = 8192, 512, 256, 512
FLOPS = 2 * B * I * OH + 2 * B * OH * OH + 2 * B * OH * H

F32 = mybir.dt.float32
BF16 = mybir.dt.bfloat16
U32 = mybir.dt.uint32
U8 = mybir.dt.uint8
FP8 = mybir.dt.float8_e4m3fn
FP8X4 = mybir.dt.float8_e4m3fn_x4
MULT = mybir.AluOpType.mult
SIGMOID = mybir.ActivationFunctionType.Sigmoid

P = 128
ROWS = B // P
STEP_ROWS = 2
STEPS = ROWS // STEP_ROWS
N = STEP_ROWS * P
GROUPS = [1, 1] + [2] * 14 + [1, 1]
CHUNKS = [1, 1, 2] + [4] * 7
FIRST_CHUNKS = 4
LOAD_LEAD = 10


def tile_lstmcell_pa_t_kernel(tc, x_bytes, x_scale, me_output, W_memi, W_memh, W_memt, mem_bias, out):
    nc = tc.nc
    x_rows = x_bytes.rearrange("(p r) k -> p r k", p=P)
    me_rows = me_output.rearrange("(p r) k -> p r k", p=P)
    out_rows = out.rearrange("(p r) n -> p r n", p=P)
    group_start = [sum(GROUPS[:g]) for g in range(len(GROUPS))]
    group_of = [g for g, n in enumerate(GROUPS) for i in range(n)]
    chunk_start = [sum(CHUNKS[:c]) for c in range(len(CHUNKS))]
    chunk_of = [c for c, n in enumerate(CHUNKS) for i in range(n)]

    with ExitStack() as ctx:
        keep = ctx.enter_context(tc.tile_pool(name="keep", bufs=1))
        work = ctx.enter_context(tc.tile_pool(name="work", bufs=3))
        psum = ctx.enter_context(tc.psum_pool(name="psum", bufs=1))
        ctx.enter_context(tc.manual_schedule())

        x_in, me_in = {}, {}

        def load_x(c):
            r0, n = chunk_start[c] * STEP_ROWS, CHUNKS[c] * STEP_ROWS
            x_in[c] = work.tile([P, n * I], U8, name="x_in", bufs=4, align_bytes=64)
            nc.sync.dma_start(
                out=x_in[c][:].rearrange("p (r k) -> p r k", k=I), in_=x_rows[:, r0 : r0 + n, :]
            )

        def load_me(c):
            r0, n = chunk_start[c] * STEP_ROWS, CHUNKS[c] * STEP_ROWS
            me_in[c] = work.tile([P, n * OH], BF16, name="me_in", bufs=4, align_bytes=64)
            nc.sync.dma_start(
                out=me_in[c][:].rearrange("p (r k) -> p r k", k=OH), in_=me_rows[:, r0 : r0 + n, :]
            )

        wi_raw = keep.tile([P, 4, OH], BF16, align_bytes=64)
        wh_raw = keep.tile([P, 4, OH], BF16, align_bytes=64)
        wt_raw = keep.tile([P, 4, H], BF16, align_bytes=64)
        scale = keep.tile([P, 4], F32, align_bytes=64)
        bias = keep.tile([P, 4], BF16, align_bytes=64)
        nc.sync.dma_start(out=scale[:], in_=x_scale.rearrange("o (p t) -> p (o t)", p=P))
        load_x(0)
        load_me(0)
        load_x(1)
        nc.sync.dma_start(out=wi_raw[:], in_=W_memi.rearrange("(p j) c -> p j c", j=4))
        nc.sync.dma_start(out=wh_raw[:], in_=W_memh.rearrange("(p j) c -> p j c", j=4))
        nc.sync.dma_start(out=bias[:], in_=mem_bias.rearrange("(p t) -> p t", t=4))
        load_me(1)
        load_x(2)
        load_me(2)
        nc.sync.dma_start(out=wt_raw[:], in_=W_memt.rearrange("(p j) c -> p j c", j=4))
        load_x(3)
        load_me(3)

        warm = keep.tile([P, 1], F32, align_bytes=64)
        nc.vector.memset(warm[:], 0.0)
        nc.scalar.activation(out=warm[:], in_=warm[:], func=SIGMOID)
        ident = keep.tile([P, P], F32, align_bytes=64)
        make_identity(nc, ident[:])

        scale_row = keep.tile([P, max(GROUPS) * STEP_ROWS * I], F32, align_bytes=64)
        bank_s = psum.tile([P, 2, N], F32, name="bank_x", bufs=2)
        for t in range(4):
            nc.tensor.transpose(
                bank_s[:, t // 2, (t % 2) * P : (t % 2 + 1) * P], scale[:, t : t + 1].to_broadcast([P, P]), ident[:]
            )
        nc.scalar.copy(
            out=scale_row[:, 0:I].rearrange("p (n h t) -> p n h t", h=2, t=2),
            in_=bank_s[:].rearrange("p h (t n) -> p n h t", t=2),
        )
        nc.vector.tensor_copy(out=scale_row[:, I : 2 * I], in_=scale_row[:, 0:I])

        wi_g = keep.tile([P, 4 * OH], BF16, align_bytes=64)
        wh_g = [keep.tile([P, 2 * OH], BF16, name="wh_g%d" % i, align_bytes=64) for i in range(2)]
        wt_g = keep.tile([P, 4 * H], BF16, align_bytes=64)
        wi_q = keep.tile([P, OH], U32, align_bytes=64)
        wi_s = keep.tile([P, OH], U8, align_bytes=64)
        wh_q = keep.tile([P, OH], U32, align_bytes=64)
        wh_s = keep.tile([P, OH], U8, align_bytes=64)
        wt_q = keep.tile([P, H], U32, align_bytes=64)
        wt_s = keep.tile([P, H], U8, align_bytes=64)

        def permuted(raw, t0, t1):
            return raw[:].rearrange("p j (m t) -> p t m j", t=4)[:, t0:t1]

        def grouped(g, nt):
            return g[:].rearrange("p (t m j) -> p t m j", t=nt, j=4)

        def quantize(q, s, g):
            nc.vector.quantize_mx(out=q.bitcast(FP8X4), scales=s, in_=g)

        xb, xm, xmq, xms, sig, gated, gq, gs = {}, {}, {}, {}, {}, {}, {}, {}
        bx, bm, ba, bb, bo = {}, {}, {}, {}, {}

        def steps(g):
            return range(group_start[g], group_start[g] + GROUPS[g]) if 0 <= g < len(GROUPS) else range(0)

        def place(s):
            return group_of[s], s - group_start[group_of[s]]

        def product_x(g):
            n = GROUPS[g] * STEP_ROWS * I
            c = chunk_of[group_start[g]]
            c0 = (group_start[g] - chunk_start[c]) * STEP_ROWS * I
            xb[g] = work.tile([P, n], BF16, name="xb", align_bytes=64)
            nc.vector.tensor_tensor(
                out=xb[g][:], in0=x_in[c][:, c0 : c0 + n].bitcast(FP8), in1=scale_row[:, 0:n], op=MULT
            )

        def transposes(bank, words):
            for a in range(STEP_ROWS):
                for u in range(2):
                    nc.tensor.transpose(
                        bank[:, u, a * P : (a + 1) * P], words[:, a * 256 + u : (a + 1) * 256 : 2], ident[:]
                    )

        def transpose_x(s):
            g, h = place(s)
            bx[s] = psum.tile([P, 2, N], F32, name="bank_x", bufs=2)
            transposes(bx[s], xb[g][:, h * 1024 : (h + 1) * 1024].bitcast(F32))

        def transpose_me(s):
            c = chunk_of[s]
            c0 = (s - chunk_start[c]) * STEP_ROWS * OH
            bm[s] = psum.tile([P, 2, N], F32, name="bank_m", bufs=2)
            transposes(bm[s], me_in[c][:, c0 : c0 + STEP_ROWS * OH].bitcast(F32))

        def copy_out(bank, dst):
            nc.scalar.copy(
                out=dst.bitcast(F32).rearrange("p (r u) -> p r u", u=2), in_=bank[:].rearrange("p u r -> p r u")
            )

        def me_cols(g):
            return GROUPS[g] * 4 * N

        def copy_me(s):
            g, h = place(s)
            if h == 0:
                xm[g] = work.tile([P, 2 * me_cols(g)], BF16, name="xm", bufs=5, align_bytes=64)
            m0 = me_cols(g) + h * 4 * N
            copy_out(bm.pop(s), xm[g][:, m0 : m0 + 4 * N])

        def copy_x(s):
            g, h = place(s)
            copy_out(bx.pop(s), xm[g][:, h * 4 * N : (h + 1) * 4 * N])

        def quantize_xm(g):
            n = 2 * GROUPS[g] * N
            xmq[g] = work.tile([P, n], U32, name="xmq", align_bytes=64)
            xms[g] = work.tile([P, n], U8, name="xms", align_bytes=64)
            quantize(xmq[g][:], xms[g][:], xm[g][:])

        def matmul1(s):
            g, h = place(s)
            ba[s] = psum.tile([P, 2, N], F32, name="bank_a", bufs=1)
            bb[s] = psum.tile([P, 2, N], F32, name="bank_b", bufs=1)
            for t in range(4):
                w = slice(t * P, (t + 1) * P)
                for i in range(2):
                    wq, ws = ((wi_q, wi_s), (wh_q, wh_s))[i]
                    c0 = (i * GROUPS[g] + h) * N
                    nc.tensor.matmul_mx(
                        out=(ba, bb)[t // 2][s][:, t % 2, :],
                        lhsT=wq[:, w].bitcast(FP8X4),
                        lhsT_scale=ws[:, w],
                        rhs=xmq[g][:, c0 : c0 + N].bitcast(FP8X4),
                        rhs_scale=xms[g][:, c0 : c0 + N],
                        start=(i == 0),
                        stop=(i == 1),
                    )

        def sigmoids(s):
            g, h = place(s)
            if h == 0:
                sig[g] = work.tile([P, GROUPS[g] * 4 * N], F32, name="sig", align_bytes=64)
            quads = sig[g][:, h * 4 * N : (h + 1) * 4 * N].rearrange("p (c t i) -> p c t i", t=4, i=4)
            for t in range(4):
                nc.scalar.activation(
                    out=quads[:, :, t, :],
                    in_=(ba, bb)[t // 2][s][:, t % 2, :].rearrange("p (c i) -> p c i", i=4),
                    func=SIGMOID,
                    bias=bias[:, t : t + 1],
                )

        def gate(g, n0, n1):
            if n0 == 0:
                gated[g] = work.tile([P, me_cols(g)], BF16, name="gated", bufs=2, align_bytes=64)
            m0 = me_cols(g)
            nc.vector.tensor_tensor(
                out=gated[g][:, 4 * n0 : 4 * n1].rearrange("p (c i t) -> p c t i", i=4, t=4),
                in0=sig[g][:, 4 * n0 : 4 * n1].rearrange("p (c t i) -> p c t i", i=4, t=4),
                in1=xm[g][:, m0 + 4 * n0 : m0 + 4 * n1].rearrange("p (c i t) -> p c t i", i=4, t=4),
                op=MULT,
            )

        def quantize_gated(g, n0, n1):
            if n0 == 0:
                gq[g] = work.tile([P, GROUPS[g] * N], U32, name="gq", align_bytes=64)
                gs[g] = work.tile([P, GROUPS[g] * N], U8, name="gs", align_bytes=64)
            quantize(gq[g][:, n0:n1], gs[g][:, n0:n1], gated[g][:, 4 * n0 : 4 * n1])

        def matmul2_row(bank_row, g, n0):
            nc.tensor.matmul_mx(
                out=bank_row,
                lhsT=gq[g][:, n0 : n0 + P].bitcast(FP8X4),
                lhsT_scale=gs[g][:, n0 : n0 + P],
                rhs=wt_q[:].bitcast(FP8X4),
                rhs_scale=wt_s[:],
                start=True,
                stop=True,
            )

        def matmul2(s):
            g, h = place(s)
            bo[s] = psum.tile([P, 2, H], F32, name="bank_o", bufs=2)
            for a in range(2):
                matmul2_row(bo[s][:, a, :], g, h * N + a * P)

        def store(s):
            t = work.tile([P, STEP_ROWS, H], F32, name="result", bufs=4, align_bytes=64)
            nc.scalar.copy(out=t[:], in_=bo.pop(s)[:])
            nc.sync.dma_start(out=out_rows[:, s * STEP_ROWS : (s + 1) * STEP_ROWS, :], in_=t[:])

        last = len(GROUPS) - 1
        next_chunk = FIRST_CHUNKS
        for j in range(-4, last + 2):
            reach = group_start[min(max(j, 0), last)]
            while next_chunk < len(CHUNKS) and chunk_start[next_chunk] <= reach + LOAD_LEAD:
                load_x(next_chunk)
                load_me(next_chunk)
                next_chunk += 1
            ahead = 0 <= j + 4 <= last
            if ahead and j != -2:
                product_x(j + 4)
            if j == -3:
                nc.vector.tensor_copy(out=grouped(wi_g, 4), in_=permuted(wi_raw, 0, 4))
            if 0 <= j < last:
                gate(j, 0, GROUPS[j] * N)
            if 0 <= j + 2 <= last:
                quantize_xm(j + 2)
            if j == -2:
                quantize(wi_q[:], wi_s[:], wi_g[:])
                product_x(j + 4)
                for i in range(2):
                    quantize(wh_q[:, i * 256 : (i + 1) * 256], wh_s[:, i * 256 : (i + 1) * 256], wh_g[i][:])
            if 0 <= j < last:
                quantize_gated(j, 0, GROUPS[j] * N)
            if j == 0:
                quantize(wt_q[:], wt_s[:], wt_g[:])
            if j == last:
                for a in range(2):
                    gate(j, a * P, (a + 1) * P)
                for a in range(2):
                    quantize_gated(j, a * P, (a + 1) * P)
                for a in range(2):
                    bank = psum.tile([P, 2, H], F32, name="bank_o", bufs=2)
                    matmul2_row(bank[:, 0, :], j, a * P)
                    res = work.tile([P, H], F32, name="result_row", bufs=2, align_bytes=64)
                    if a == 0:
                        nc.scalar.copy(out=res[:], in_=bank[:, 0, :])
                    else:
                        nc.vector.tensor_copy(out=res[:], in_=bank[:, 0, :])
                    nc.sync.dma_start(out=out_rows[:, ROWS - 2 + a, :], in_=res[:])
            m1, t, m2 = list(steps(j + 1)), list(steps(j + 3)), list(steps(j - 1)) if j <= last else []
            for h in range(2):
                for s in m1[h : h + 1]:
                    matmul1(s)
                    sigmoids(s)
                for s in m2[h : h + 1]:
                    matmul2(s)
                    store(s)
                for s in t[h : h + 1]:
                    transpose_me(s)
                    copy_me(s)
                    if j == -3:
                        nc.scalar.copy(out=scale_row[:, 2 * I :], in_=scale_row[:, 0 : 2 * I])
                        nc.scalar.copy(out=grouped(wh_g[0], 2), in_=permuted(wh_raw, 0, 2))
                    transpose_x(s)
                    copy_x(s)
            if j == -3:
                nc.scalar.copy(out=grouped(wh_g[1], 2), in_=permuted(wh_raw, 2, 4))
            if j == -1:
                nc.scalar.copy(
                    out=wt_g[:].rearrange("p (n j) -> p n j", j=4), in_=wt_raw[:].rearrange("p j n -> p n j")
                )
